import numpy as np
import ml_dtypes


def mxq(x, axis, fmt="e4m3"):
    dtype, down = {"e4m3": (ml_dtypes.float8_e4m3fn, 7), "e5m2": (ml_dtypes.float8_e5m2, 14)}[fmt]
    v = np.moveaxis(np.asarray(x, np.float32).astype(ml_dtypes.bfloat16).astype(np.float64), axis, -1)
    blocks = v.reshape(v.shape[:-1] + (-1, 32))
    amax = np.abs(blocks).max(-1, keepdims=True)
    byte = np.maximum(np.where(amax > 0, np.frexp(amax)[1] - 1 + 127, 0) - down, 1)
    scale = np.exp2(byte - 127.0)
    codes = (blocks / scale).astype(np.float32).astype(dtype).astype(np.float64)
    return np.moveaxis((codes * scale).reshape(v.shape), -1, axis)


WIDE = False


def mx_kscale(k):
    if not WIDE:
        return np.ones(k)
    levels = np.array([10, -10, 5, -5, 0])
    a = np.random.permutation(np.resize(levels, k // 512 * 4)).reshape(k // 512, 4)
    idx = np.arange(k)
    return np.exp2(a[idx // 512, idx % 128 // 32])


BF16 = ml_dtypes.bfloat16


def bf(x):
    return np.asarray(x, np.float32).astype(BF16)


def f64(x):
    return np.asarray(x).astype(np.float64)


B, N, K, H, C_E, M = 2, 64, 16, 1024, 1024, 1024
SCALE = 30.0


def setup_inputs():
    s = mx_kscale(M)
    return {"h2": bf(np.random.standard_normal((B, N, K, M)) * 0.65 * s),
            "h_V": bf(np.random.standard_normal((B, N, H))),
            "mask_attend": bf(np.random.uniform(size=(B, N, K)) < 0.9),
            "W3_w": bf(np.random.standard_normal((M, H)) * 4.0 / np.sqrt(M) / s[:, None]),
            "W3_b": bf(np.random.standard_normal(H) * 0.1)}


def reference(h2, h_V, mask_attend, W3_w, W3_b):
    h_message = (mxq(f64(h2), 3, "e4m3") @ mxq(f64(W3_w), 0, "e4m3")) + f64(W3_b)
    h_message = f64(mask_attend)[..., None] * h_message
    dh = np.sum(h_message, axis=-2) / SCALE
    return f64(h_V) + dh

@@ -1,0 +1,185 @@
+from contextlib import ExitStack
+
+import concourse.mybir as mybir
+from concourse.masks import make_identity
+
+F32 = mybir.dt.float32
+BF16 = mybir.dt.bfloat16
+U32 = mybir.dt.uint32
+U8 = mybir.dt.uint8
+FP8X4 = mybir.dt.float8_e4m3fn_x4
+ALU = mybir.AluOpType
+COPY = mybir.ActivationFunctionType.Copy
+
+P = 128
+EDGES = 16
+K = 1024
+H = 1024
+PACK = 4
+K_PASS = P * PACK
+PASSES = K // K_PASS
+PLANES = K // (2 * P)
+N_TILE = 512
+HALVES = H // N_TILE
+CHUNK = 4
+CHUNKS = EDGES // CHUNK
+SCALE = 30.0
+
+FLOPS = 2 * P * EDGES * K * H
+
+
+def tile_declayerj_pb_kernel(tc, h2, h_V, mask_attend, W3_w, W3_b, out):
+    nc = tc.nc
+    h2_rows = h2.rearrange("b n e k -> (b n) (e k)")
+    mask_rows = mask_attend.rearrange("b n e -> (b n) e")
+    hv_rows = h_V.rearrange("b n h -> (b n) h")
+    out_rows = out.rearrange("b n h -> (b n) h")
+
+    with ExitStack() as ctx:
+        keep = ctx.enter_context(tc.tile_pool(name="keep", bufs=1))
+        acc_pool = ctx.enter_context(tc.psum_pool(name="acc", bufs=1))
+        bias_pool = ctx.enter_context(tc.psum_pool(name="bias", bufs=1))
+        turn_pool = ctx.enter_context(tc.psum_pool(name="turn", bufs=CHUNK))
+
+        mask_bf = keep.tile([P, EDGES], BF16)
+        nc.sync.dma_start(out=mask_bf[:], in_=mask_rows)
+
+        bias_rows = keep.tile([P, H], BF16)
+        nc.vector.memset(bias_rows[:], 0.0)
+        nc.sync.dma_start(out=bias_rows[0:1, :], in_=W3_b.unsqueeze(0))
+
+        w_raw = [keep.tile([P, PASSES, PACK, N_TILE], BF16, name="w_raw%d" % half) for half in range(HALVES)]
+        h2_in = [keep.tile([P, CHUNK * K], BF16, name="h2_in%d" % c) for c in range(CHUNKS)]
+
+        def load_w(half, g):
+            for u in range(2):
+                first = K_PASS * g + 2 * P * u
+                nc.sync.dma_start(
+                    out=w_raw[half][:, g, 2 * u : 2 * u + 2, :],
+                    in_=W3_w[first : first + 2 * P, N_TILE * half : N_TILE * (half + 1)].rearrange(
+                        "(p v) c -> p v c", v=2
+                    ),
+                )
+
+        def load_h2(c):
+            nc.sync.dma_start(out=h2_in[c][:], in_=h2_rows[:, CHUNK * K * c : CHUNK * K * (c + 1)])
+
+        load_w(0, 0)
+        load_h2(0)
+        load_w(0, 1)
+        for c in range(1, CHUNKS):
+            load_h2(c)
+        hv = keep.tile([P, H], BF16)
+        nc.sync.dma_start(out=hv[:], in_=hv_rows)
+        load_w(1, 0)
+        load_w(1, 1)
+
+        ident = keep.tile([P, P], F32)
+        make_identity(nc, ident[:])
+        mask_f32 = keep.tile([P, EDGES], F32)
+        nc.vector.tensor_copy(out=mask_f32[:], in_=mask_bf[:])
+        gates = keep.tile([P, EDGES, P], F32)
+        for e in range(EDGES):
+            nc.scalar.activation(out=gates[:, e, :], in_=ident[:], func=COPY, scale=mask_f32[:, e : e + 1])
+
+        count = keep.tile([P, 1], F32)
+        nc.vector.reduce_sum(out=count[:], in_=mask_f32[:], axis=mybir.AxisListType.X)
+        count30 = keep.tile([P, 1], F32)
+        nc.vector.tensor_scalar(out=count30[:], in0=count[:], scalar1=1.0 / SCALE, scalar2=None, op0=ALU.mult)
+
+        ones = keep.tile([P, P], BF16)
+        nc.vector.memset(ones[:], 1.0)
+        bias_all = [bias_pool.tile([P, N_TILE], F32, name="bias_all%d" % half) for half in range(HALVES)]
+        for half in range(HALVES):
+            nc.tensor.matmul(
+                out=bias_all[half][:],
+                lhsT=ones[:],
+                rhs=bias_rows[:, N_TILE * half : N_TILE * (half + 1)],
+                start=True,
+                stop=True,
+            )
+
+        w_grouped = [
+            keep.tile([P, PASSES, N_TILE, PACK], BF16, name="w_grouped%d" % half, align_bytes=64)
+            for half in range(HALVES)
+        ]
+        w_codes = keep.tile([P, HALVES, PASSES, N_TILE], U32, align_bytes=64)
+        w_scales = keep.tile([P, HALVES, PASSES, N_TILE], U8, align_bytes=64)
+
+        def quantise_w(half):
+            for g in range(PASSES):
+                nc.vector.tensor_copy(
+                    out=w_grouped[half][:, g].rearrange("p (c i) t -> p c t i", i=4),
+                    in_=w_raw[half][:, g].rearrange("p t (c i) -> p c t i", i=4),
+                )
+            for g in range(PASSES):
+                nc.vector.quantize_mx(
+                    out=w_codes[:, half, g, :].bitcast(FP8X4),
+                    scales=w_scales[:, half, g, :],
+                    in_=w_grouped[half][:, g].rearrange("p c t -> p (c t)"),
+                )
+
+        h2_grouped = [keep.tile([P, CHUNK * K], BF16, name="h2_grouped%d" % c, align_bytes=64) for c in range(CHUNKS)]
+        h2_codes = keep.tile([P, EDGES, PASSES * P], U32, align_bytes=64)
+        h2_scales = keep.tile([P, EDGES, PASSES * P], U8, align_bytes=64)
+
+        def quantise_h2(c):
+            words_in = h2_in[c][:].bitcast(F32)
+            words_out = h2_grouped[c][:].bitcast(F32).rearrange(
+                "p (e g n u) -> p e g n u", e=CHUNK, g=PASSES, u=2
+            )
+            for i in range(CHUNK):
+                e = CHUNK * c + i
+                turned = turn_pool.tile([P, PLANES, P], F32)
+                for j in range(PLANES):
+                    first = (PLANES * i + j) * P
+                    nc.tensor.transpose(turned[:, j, :], words_in[:, first : first + P], gates[:, e, :])
+                nc.scalar.copy(out=words_out[:, i], in_=turned[:].rearrange("p (g u) n -> p g n u", u=2))
+                nc.vector.quantize_mx(
+                    out=h2_codes[:, e, :].bitcast(FP8X4),
+                    scales=h2_scales[:, e, :],
+                    in_=h2_grouped[c][:, K * i : K * (i + 1)],
+                )
+
+        acc = [acc_pool.tile([P, N_TILE], F32, name="acc%d" % half) for half in range(HALVES)]
+
+        def multiply(half, edges):
+            for g in range(PASSES):
+                for e in edges:
+                    nc.tensor.matmul_mx(
+                        out=acc[half][:],
+                        lhsT=h2_codes[:, e, P * g : P * (g + 1)].bitcast(FP8X4),
+                        lhsT_scale=h2_scales[:, e, P * g : P * (g + 1)],
+                        rhs=w_codes[:, half, g, :].bitcast(FP8X4),
+                        rhs_scale=w_scales[:, half, g, :],
+                        start=(e == 0 and g == 0),
+                        stop=(e == EDGES - 1 and g == PASSES - 1),
+                    )
+
+        base = keep.tile([P, H], F32)
+        result = keep.tile([P, H], F32)
+
+        def finish(half):
+            cols = slice(N_TILE * half, N_TILE * (half + 1))
+            nc.vector.scalar_tensor_tensor(
+                out=result[:, cols], in0=acc[half][:], scalar=1.0 / SCALE, in1=base[:, cols], op0=ALU.mult, op1=ALU.add
+            )
+            nc.sync.dma_start(out=out_rows[:, cols], in_=result[:, cols])
+
+        quantise_w(0)
+        quantise_h2(0)
+        for c in range(CHUNKS):
+            if c + 1 < CHUNKS:
+                quantise_h2(c + 1)
+            multiply(0, range(CHUNK * c, CHUNK * (c + 1)))
+
+        quantise_w(1)
+        for half in range(HALVES):
+            cols = slice(N_TILE * half, N_TILE * (half + 1))
+            nc.vector.scalar_tensor_tensor(
+                out=base[:, cols], in0=bias_all[half][:], scalar=count30[:, 0:1], in1=hv[:, cols], op0=ALU.mult, op1=ALU.add
+            )
+        finish(0)
+
+        multiply(1, range(EDGES))
+        finish(1)

@@ -9,7 +9,6 @@ U32 = mybir.dt.uint32
 U8 = mybir.dt.uint8
 FP8X4 = mybir.dt.float8_e4m3fn_x4
 ALU = mybir.AluOpType
-COPY = mybir.ActivationFunctionType.Copy
 
 P = 128
 EDGES = 16
@@ -23,6 +22,7 @@ N_TILE = 512
 HALVES = H // N_TILE
 CHUNK = 4
 CHUNKS = EDGES // CHUNK
+LOAD = 2
 SCALE = 30.0
 
 FLOPS = 2 * P * EDGES * K * H
@@ -40,6 +40,7 @@ def tile_declayerj_pb_kernel(tc, h2, h_V, mask_attend, W3_w, W3_b, out):
         acc_pool = ctx.enter_context(tc.psum_pool(name="acc", bufs=1))
         bias_pool = ctx.enter_context(tc.psum_pool(name="bias", bufs=1))
         turn_pool = ctx.enter_context(tc.psum_pool(name="turn", bufs=CHUNK))
+        ctx.enter_context(tc.manual_schedule())
 
         mask_bf = keep.tile([P, EDGES], BF16)
         nc.sync.dma_start(out=mask_bf[:], in_=mask_rows)
@@ -47,6 +48,8 @@ def tile_declayerj_pb_kernel(tc, h2, h_V, mask_attend, W3_w, W3_b, out):
         bias_rows = keep.tile([P, H], BF16)
         nc.vector.memset(bias_rows[:], 0.0)
         nc.sync.dma_start(out=bias_rows[0:1, :], in_=W3_b.unsqueeze(0))
+        ones = keep.tile([P, P], BF16)
+        nc.vector.memset(ones[:], 1.0)
 
         w_raw = [keep.tile([P, PASSES, PACK, N_TILE], BF16, name="w_raw%d" % half) for half in range(HALVES)]
         h2_in = [keep.tile([P, CHUNK * K], BF16, name="h2_in%d" % c) for c in range(CHUNKS)]
@@ -62,33 +65,40 @@ def tile_declayerj_pb_kernel(tc, h2, h_V, mask_attend, W3_w, W3_b, out):
                 )
 
         def load_h2(c):
-            nc.sync.dma_start(out=h2_in[c][:], in_=h2_rows[:, CHUNK * K * c : CHUNK * K * (c + 1)])
+            for first in range(0, CHUNK * K, LOAD * K):
+                nc.sync.dma_start(
+                    out=h2_in[c][:, first : first + LOAD * K],
+                    in_=h2_rows[:, CHUNK * K * c + first : CHUNK * K * c + first + LOAD * K],
+                )
 
-        load_w(0, 0)
-        load_h2(0)
-        load_w(0, 1)
-        for c in range(1, CHUNKS):
+        for g in range(PASSES):
+            load_w(0, g)
+        for c in range(CHUNKS):
             load_h2(c)
+            if 0 <= c - 1 < PASSES:
+                load_w(1, c - 1)
         hv = keep.tile([P, H], BF16)
         nc.sync.dma_start(out=hv[:], in_=hv_rows)
-        load_w(1, 0)
-        load_w(1, 1)
 
         ident = keep.tile([P, P], F32)
         make_identity(nc, ident[:])
         mask_f32 = keep.tile([P, EDGES], F32)
         nc.vector.tensor_copy(out=mask_f32[:], in_=mask_bf[:])
         gates = keep.tile([P, EDGES, P], F32)
-        for e in range(EDGES):
-            nc.scalar.activation(out=gates[:, e, :], in_=ident[:], func=COPY, scale=mask_f32[:, e : e + 1])
+
+        def make_gates(c):
+            for e in range(CHUNK * c, CHUNK * (c + 1)):
+                nc.vector.tensor_scalar(
+                    out=gates[:, e, :], in0=ident[:], scalar1=mask_f32[:, e : e + 1], scalar2=None, op0=ALU.mult
+                )
+
+        make_gates(0)
 
         count = keep.tile([P, 1], F32)
         nc.vector.reduce_sum(out=count[:], in_=mask_f32[:], axis=mybir.AxisListType.X)
         count30 = keep.tile([P, 1], F32)
         nc.vector.tensor_scalar(out=count30[:], in0=count[:], scalar1=1.0 / SCALE, scalar2=None, op0=ALU.mult)
 
-        ones = keep.tile([P, P], BF16)
-        nc.vector.memset(ones[:], 1.0)
         bias_all = [bias_pool.tile([P, N_TILE], F32, name="bias_all%d" % half) for half in range(HALVES)]
         for half in range(HALVES):
             nc.tensor.matmul(
@@ -106,18 +116,18 @@ def tile_declayerj_pb_kernel(tc, h2, h_V, mask_attend, W3_w, W3_b, out):
         w_codes = keep.tile([P, HALVES, PASSES, N_TILE], U32, align_bytes=64)
         w_scales = keep.tile([P, HALVES, PASSES, N_TILE], U8, align_bytes=64)
 
-        def quantise_w(half):
-            for g in range(PASSES):
-                nc.vector.tensor_copy(
-                    out=w_grouped[half][:, g].rearrange("p (c i) t -> p c t i", i=4),
-                    in_=w_raw[half][:, g].rearrange("p t (c i) -> p c t i", i=4),
-                )
-            for g in range(PASSES):
-                nc.vector.quantize_mx(
-                    out=w_codes[:, half, g, :].bitcast(FP8X4),
-                    scales=w_scales[:, half, g, :],
-                    in_=w_grouped[half][:, g].rearrange("p c t -> p (c t)"),
-                )
+        def regroup_w(half, g):
+            nc.vector.tensor_copy(
+                out=w_grouped[half][:, g].rearrange("p (c i) t -> p c t i", i=4),
+                in_=w_raw[half][:, g].rearrange("p t (c i) -> p c t i", i=4),
+            )
+
+        def quantise_w(half, g):
+            nc.vector.quantize_mx(
+                out=w_codes[:, half, g, :].bitcast(FP8X4),
+                scales=w_scales[:, half, g, :],
+                in_=w_grouped[half][:, g].rearrange("p c t -> p (c t)"),
+            )
 
         h2_grouped = [keep.tile([P, CHUNK * K], BF16, name="h2_grouped%d" % c, align_bytes=64) for c in range(CHUNKS)]
         h2_codes = keep.tile([P, EDGES, PASSES * P], U32, align_bytes=64)
@@ -144,8 +154,8 @@ def tile_declayerj_pb_kernel(tc, h2, h_V, mask_attend, W3_w, W3_b, out):
         acc = [acc_pool.tile([P, N_TILE], F32, name="acc%d" % half) for half in range(HALVES)]
 
         def multiply(half, edges):
-            for g in range(PASSES):
-                for e in edges:
+            for e in edges:
+                for g in range(PASSES):
                     nc.tensor.matmul_mx(
                         out=acc[half][:],
                         lhsT=h2_codes[:, e, P * g : P * (g + 1)].bitcast(FP8X4),
@@ -166,14 +176,20 @@ def tile_declayerj_pb_kernel(tc, h2, h_V, mask_attend, W3_w, W3_b, out):
             )
             nc.sync.dma_start(out=out_rows[:, cols], in_=result[:, cols])
 
-        quantise_w(0)
-        quantise_h2(0)
+        for g in range(PASSES):
+            regroup_w(0, g)
+        for g in range(PASSES):
+            quantise_w(0, g)
         for c in range(CHUNKS):
+            quantise_h2(c)
+            if 0 <= c - 1 < PASSES:
+                regroup_w(1, c - 1)
             if c + 1 < CHUNKS:
-                quantise_h2(c + 1)
+                make_gates(c + 1)
+            if 0 <= c - 1 < PASSES:
+                quantise_w(1, c - 1)
             multiply(0, range(CHUNK * c, CHUNK * (c + 1)))
 
-        quantise_w(1)
         for half in range(HALVES):
             cols = slice(N_TILE * half, N_TILE * (half + 1))
             nc.vector.scalar_tensor_tensor(

@@ -20,9 +20,11 @@ PASSES = K // K_PASS
 PLANES = K // (2 * P)
 N_TILE = 512
 HALVES = H // N_TILE
+GROUPS = ((0, 512), (512, 256), (768, 256))
 CHUNK = 4
 CHUNKS = EDGES // CHUNK
 LOAD = 2
+LAG = 2
 SCALE = 30.0
 
 FLOPS = 2 * P * EDGES * K * H
@@ -38,7 +40,6 @@ def tile_declayerj_pb_kernel(tc, h2, h_V, mask_attend, W3_w, W3_b, out):
     with ExitStack() as ctx:
         keep = ctx.enter_context(tc.tile_pool(name="keep", bufs=1))
         acc_pool = ctx.enter_context(tc.psum_pool(name="acc", bufs=1))
-        bias_pool = ctx.enter_context(tc.psum_pool(name="bias", bufs=1))
         turn_pool = ctx.enter_context(tc.psum_pool(name="turn", bufs=CHUNK))
         ctx.enter_context(tc.manual_schedule())
 
@@ -47,7 +48,7 @@ def tile_declayerj_pb_kernel(tc, h2, h_V, mask_attend, W3_w, W3_b, out):
 
         bias_rows = keep.tile([P, H], BF16)
         nc.vector.memset(bias_rows[:], 0.0)
-        nc.sync.dma_start(out=bias_rows[0:1, :], in_=W3_b.unsqueeze(0))
+        nc.scalar.dma_start(out=bias_rows[0:1, :], in_=W3_b.unsqueeze(0))
         ones = keep.tile([P, P], BF16)
         nc.vector.memset(ones[:], 1.0)
 
@@ -99,7 +100,7 @@ def tile_declayerj_pb_kernel(tc, h2, h_V, mask_attend, W3_w, W3_b, out):
         count30 = keep.tile([P, 1], F32)
         nc.vector.tensor_scalar(out=count30[:], in0=count[:], scalar1=1.0 / SCALE, scalar2=None, op0=ALU.mult)
 
-        bias_all = [bias_pool.tile([P, N_TILE], F32, name="bias_all%d" % half) for half in range(HALVES)]
+        bias_all = [acc_pool.tile([P, N_TILE], F32, name="bias_all%d" % half, tag="late%d" % half) for half in range(HALVES)]
         for half in range(HALVES):
             nc.tensor.matmul(
                 out=bias_all[half][:],
@@ -113,8 +114,8 @@ def tile_declayerj_pb_kernel(tc, h2, h_V, mask_attend, W3_w, W3_b, out):
             keep.tile([P, PASSES, N_TILE, PACK], BF16, name="w_grouped%d" % half, align_bytes=64)
             for half in range(HALVES)
         ]
-        w_codes = keep.tile([P, HALVES, PASSES, N_TILE], U32, align_bytes=64)
-        w_scales = keep.tile([P, HALVES, PASSES, N_TILE], U8, align_bytes=64)
+        w_codes = keep.tile([P, PASSES, H], U32, align_bytes=64)
+        w_scales = keep.tile([P, PASSES, H], U8, align_bytes=64)
 
         def regroup_w(half, g):
             nc.vector.tensor_copy(
@@ -123,9 +124,10 @@ def tile_declayerj_pb_kernel(tc, h2, h_V, mask_attend, W3_w, W3_b, out):
             )
 
         def quantise_w(half, g):
+            cols = slice(N_TILE * half, N_TILE * (half + 1))
             nc.vector.quantize_mx(
-                out=w_codes[:, half, g, :].bitcast(FP8X4),
-                scales=w_scales[:, half, g, :],
+                out=w_codes[:, g, cols].bitcast(FP8X4),
+                scales=w_scales[:, g, cols],
                 in_=w_grouped[half][:, g].rearrange("p c t -> p (c t)"),
             )
 
@@ -151,17 +153,16 @@ def tile_declayerj_pb_kernel(tc, h2, h_V, mask_attend, W3_w, W3_b, out):
                     in_=h2_grouped[c][:, K * i : K * (i + 1)],
                 )
 
-        acc = [acc_pool.tile([P, N_TILE], F32, name="acc%d" % half) for half in range(HALVES)]
-
-        def multiply(half, edges):
+        def multiply(acc, group, edges):
+            first, width = group
             for e in edges:
                 for g in range(PASSES):
                     nc.tensor.matmul_mx(
-                        out=acc[half][:],
+                        out=acc[:],
                         lhsT=h2_codes[:, e, P * g : P * (g + 1)].bitcast(FP8X4),
                         lhsT_scale=h2_scales[:, e, P * g : P * (g + 1)],
-                        rhs=w_codes[:, half, g, :].bitcast(FP8X4),
-                        rhs_scale=w_scales[:, half, g, :],
+                        rhs=w_codes[:, g, first : first + width].bitcast(FP8X4),
+                        rhs_scale=w_scales[:, g, first : first + width],
                         start=(e == 0 and g == 0),
                         stop=(e == EDGES - 1 and g == PASSES - 1),
                     )
@@ -169,10 +170,11 @@ def tile_declayerj_pb_kernel(tc, h2, h_V, mask_attend, W3_w, W3_b, out):
         base = keep.tile([P, H], F32)
         result = keep.tile([P, H], F32)
 
-        def finish(half):
-            cols = slice(N_TILE * half, N_TILE * (half + 1))
+        def finish(acc, group):
+            first, width = group
+            cols = slice(first, first + width)
             nc.vector.scalar_tensor_tensor(
-                out=result[:, cols], in0=acc[half][:], scalar=1.0 / SCALE, in1=base[:, cols], op0=ALU.mult, op1=ALU.add
+                out=result[:, cols], in0=acc[:], scalar=1.0 / SCALE, in1=base[:, cols], op0=ALU.mult, op1=ALU.add
             )
             nc.sync.dma_start(out=out_rows[:, cols], in_=result[:, cols])
 
@@ -180,22 +182,25 @@ def tile_declayerj_pb_kernel(tc, h2, h_V, mask_attend, W3_w, W3_b, out):
             regroup_w(0, g)
         for g in range(PASSES):
             quantise_w(0, g)
+        acc_first = acc_pool.tile([P, GROUPS[0][1]], F32)
         for c in range(CHUNKS):
+            if c + 1 < CHUNKS:
+                make_gates(c + 1)
             quantise_h2(c)
             if 0 <= c - 1 < PASSES:
                 regroup_w(1, c - 1)
-            if c + 1 < CHUNKS:
-                make_gates(c + 1)
-            if 0 <= c - 1 < PASSES:
                 quantise_w(1, c - 1)
-            multiply(0, range(CHUNK * c, CHUNK * (c + 1)))
+            multiply(acc_first, GROUPS[0], range(max(0, CHUNK * c - LAG), CHUNK * (c + 1) - LAG))
+        multiply(acc_first, GROUPS[0], range(EDGES - LAG, EDGES))
 
         for half in range(HALVES):
             cols = slice(N_TILE * half, N_TILE * (half + 1))
             nc.vector.scalar_tensor_tensor(
                 out=base[:, cols], in0=bias_all[half][:], scalar=count30[:, 0:1], in1=hv[:, cols], op0=ALU.mult, op1=ALU.add
             )
-        finish(0)
+        finish(acc_first, GROUPS[0])
 
-        multiply(1, range(EDGES))
-        finish(1)
+        for late, group in enumerate(GROUPS[1:]):
+            acc_late = acc_pool.tile([P, group[1]], F32, tag="late%d" % late)
+            multiply(acc_late, group, range(EDGES))
+            finish(acc_late, group)

@@ -46,12 +46,6 @@ def tile_declayerj_pb_kernel(tc, h2, h_V, mask_attend, W3_w, W3_b, out):
         mask_bf = keep.tile([P, EDGES], BF16)
         nc.sync.dma_start(out=mask_bf[:], in_=mask_rows)
 
-        bias_rows = keep.tile([P, H], BF16)
-        nc.vector.memset(bias_rows[:], 0.0)
-        nc.scalar.dma_start(out=bias_rows[0:1, :], in_=W3_b.unsqueeze(0))
-        ones = keep.tile([P, P], BF16)
-        nc.vector.memset(ones[:], 1.0)
-
         w_raw = [keep.tile([P, PASSES, PACK, N_TILE], BF16, name="w_raw%d" % half) for half in range(HALVES)]
         h2_in = [keep.tile([P, CHUNK * K], BF16, name="h2_in%d" % c) for c in range(CHUNKS)]
 
@@ -80,6 +74,8 @@ def tile_declayerj_pb_kernel(tc, h2, h_V, mask_attend, W3_w, W3_b, out):
                 load_w(1, c - 1)
         hv = keep.tile([P, H], BF16)
         nc.sync.dma_start(out=hv[:], in_=hv_rows)
+        bias_all = keep.tile([P, H], BF16)
+        nc.sync.dma_start(out=bias_all[:], in_=W3_b.partition_broadcast(P))
 
         ident = keep.tile([P, P], F32)
         make_identity(nc, ident[:])
@@ -99,16 +95,6 @@ def tile_declayerj_pb_kernel(tc, h2, h_V, mask_attend, W3_w, W3_b, out):
         nc.vector.reduce_sum(out=count[:], in_=mask_f32[:], axis=mybir.AxisListType.X)
         count30 = keep.tile([P, 1], F32)
         nc.vector.tensor_scalar(out=count30[:], in0=count[:], scalar1=1.0 / SCALE, scalar2=None, op0=ALU.mult)
-
-        bias_all = [acc_pool.tile([P, N_TILE], F32, name="bias_all%d" % half, tag="late%d" % half) for half in range(HALVES)]
-        for half in range(HALVES):
-            nc.tensor.matmul(
-                out=bias_all[half][:],
-                lhsT=ones[:],
-                rhs=bias_rows[:, N_TILE * half : N_TILE * (half + 1)],
-                start=True,
-                stop=True,
-            )
 
         w_grouped = [
             keep.tile([P, PASSES, N_TILE, PACK], BF16, name="w_grouped%d" % half, align_bytes=64)
@@ -193,14 +179,12 @@ def tile_declayerj_pb_kernel(tc, h2, h_V, mask_attend, W3_w, W3_b, out):
             multiply(acc_first, GROUPS[0], range(max(0, CHUNK * c - LAG), CHUNK * (c + 1) - LAG))
         multiply(acc_first, GROUPS[0], range(EDGES - LAG, EDGES))
 
-        for half in range(HALVES):
-            cols = slice(N_TILE * half, N_TILE * (half + 1))
-            nc.vector.scalar_tensor_tensor(
-                out=base[:, cols], in0=bias_all[half][:], scalar=count30[:, 0:1], in1=hv[:, cols], op0=ALU.mult, op1=ALU.add
-            )
+        nc.vector.scalar_tensor_tensor(
+            out=base[:], in0=bias_all[:], scalar=count30[:, 0:1], in1=hv[:], op0=ALU.mult, op1=ALU.add
+        )
         finish(acc_first, GROUPS[0])
 
-        for late, group in enumerate(GROUPS[1:]):
-            acc_late = acc_pool.tile([P, group[1]], F32, tag="late%d" % late)
+        for group in GROUPS[1:]:
+            acc_late = acc_pool.tile([P, group[1]], F32, name="acc_from%d" % group[0])
             multiply(acc_late, group, range(EDGES))
             finish(acc_late, group)

@@ -41,10 +41,15 @@ def tile_declayerj_pb_kernel(tc, h2, h_V, mask_attend, W3_w, W3_b, out):
         keep = ctx.enter_context(tc.tile_pool(name="keep", bufs=1))
         acc_pool = ctx.enter_context(tc.psum_pool(name="acc", bufs=1))
         turn_pool = ctx.enter_context(tc.psum_pool(name="turn", bufs=CHUNK))
-        ctx.enter_context(tc.manual_schedule())
 
         mask_bf = keep.tile([P, EDGES], BF16)
         nc.sync.dma_start(out=mask_bf[:], in_=mask_rows)
+
+        bias_rows = keep.tile([P, H], BF16)
+        nc.vector.memset(bias_rows[:], 0.0)
+        nc.scalar.dma_start(out=bias_rows[0:1, :], in_=W3_b.unsqueeze(0))
+        ones = keep.tile([P, P], BF16)
+        nc.vector.memset(ones[:], 1.0)
 
         w_raw = [keep.tile([P, PASSES, PACK, N_TILE], BF16, name="w_raw%d" % half) for half in range(HALVES)]
         h2_in = [keep.tile([P, CHUNK * K], BF16, name="h2_in%d" % c) for c in range(CHUNKS)]
@@ -74,8 +79,6 @@ def tile_declayerj_pb_kernel(tc, h2, h_V, mask_attend, W3_w, W3_b, out):
                 load_w(1, c - 1)
         hv = keep.tile([P, H], BF16)
         nc.sync.dma_start(out=hv[:], in_=hv_rows)
-        bias_all = keep.tile([P, H], BF16)
-        nc.sync.dma_start(out=bias_all[:], in_=W3_b.partition_broadcast(P))
 
         ident = keep.tile([P, P], F32)
         make_identity(nc, ident[:])
@@ -95,6 +98,16 @@ def tile_declayerj_pb_kernel(tc, h2, h_V, mask_attend, W3_w, W3_b, out):
         nc.vector.reduce_sum(out=count[:], in_=mask_f32[:], axis=mybir.AxisListType.X)
         count30 = keep.tile([P, 1], F32)
         nc.vector.tensor_scalar(out=count30[:], in0=count[:], scalar1=1.0 / SCALE, scalar2=None, op0=ALU.mult)
+
+        bias_all = [acc_pool.tile([P, N_TILE], F32, name="bias_all%d" % half, tag="late%d" % half) for half in range(HALVES)]
+        for half in range(HALVES):
+            nc.tensor.matmul(
+                out=bias_all[half][:],
+                lhsT=ones[:],
+                rhs=bias_rows[:, N_TILE * half : N_TILE * (half + 1)],
+                start=True,
+                stop=True,
+            )
 
         w_grouped = [
             keep.tile([P, PASSES, N_TILE, PACK], BF16, name="w_grouped%d" % half, align_bytes=64)
@@ -179,12 +192,14 @@ def tile_declayerj_pb_kernel(tc, h2, h_V, mask_attend, W3_w, W3_b, out):
             multiply(acc_first, GROUPS[0], range(max(0, CHUNK * c - LAG), CHUNK * (c + 1) - LAG))
         multiply(acc_first, GROUPS[0], range(EDGES - LAG, EDGES))
 
-        nc.vector.scalar_tensor_tensor(
-            out=base[:], in0=bias_all[:], scalar=count30[:, 0:1], in1=hv[:], op0=ALU.mult, op1=ALU.add
-        )
+        for half in range(HALVES):
+            cols = slice(N_TILE * half, N_TILE * (half + 1))
+            nc.vector.scalar_tensor_tensor(
+                out=base[:, cols], in0=bias_all[half][:], scalar=count30[:, 0:1], in1=hv[:, cols], op0=ALU.mult, op1=ALU.add
+            )
         finish(acc_first, GROUPS[0])
 
-        for group in GROUPS[1:]:
-            acc_late = acc_pool.tile([P, group[1]], F32, name="acc_from%d" % group[0])
+        for late, group in enumerate(GROUPS[1:]):
+            acc_late = acc_pool.tile([P, group[1]], F32, tag="late%d" % late)
             multiply(acc_late, group, range(EDGES))
             finish(acc_late, group)

from contextlib import ExitStack

import concourse.mybir as mybir
from concourse.masks import make_identity

F32 = mybir.dt.float32
BF16 = mybir.dt.bfloat16
U32 = mybir.dt.uint32
U8 = mybir.dt.uint8
FP8X4 = mybir.dt.float8_e4m3fn_x4
ALU = mybir.AluOpType

P = 128
EDGES = 16
K = 1024
H = 1024
PACK = 4
K_PASS = P * PACK
PASSES = K // K_PASS
PLANES = K // (2 * P)
N_TILE = 512
HALVES = H // N_TILE
GROUPS = ((0, 512), (512, 256), (768, 256))
CHUNK = 4
CHUNKS = EDGES // CHUNK
LOAD = 2
LAG = 2
SCALE = 30.0

FLOPS = 2 * P * EDGES * K * H


def tile_declayerj_pb_kernel(tc, h2, h_V, mask_attend, W3_w, W3_b, out):
    nc = tc.nc
    h2_rows = h2.rearrange("b n e k -> (b n) (e k)")
    mask_rows = mask_attend.rearrange("b n e -> (b n) e")
    hv_rows = h_V.rearrange("b n h -> (b n) h")
    out_rows = out.rearrange("b n h -> (b n) h")

    with ExitStack() as ctx:
        keep = ctx.enter_context(tc.tile_pool(name="keep", bufs=1))
        acc_pool = ctx.enter_context(tc.psum_pool(name="acc", bufs=1))
        turn_pool = ctx.enter_context(tc.psum_pool(name="turn", bufs=CHUNK))

        mask_bf = keep.tile([P, EDGES], BF16)
        nc.sync.dma_start(out=mask_bf[:], in_=mask_rows)

        bias_rows = keep.tile([P, H], BF16)
        nc.vector.memset(bias_rows[:], 0.0)
        nc.scalar.dma_start(out=bias_rows[0:1, :], in_=W3_b.unsqueeze(0))
        ones = keep.tile([P, P], BF16)
        nc.vector.memset(ones[:], 1.0)

        w_raw = [keep.tile([P, PASSES, PACK, N_TILE], BF16, name="w_raw%d" % half) for half in range(HALVES)]
        h2_in = [keep.tile([P, CHUNK * K], BF16, name="h2_in%d" % c) for c in range(CHUNKS)]

        def load_w(half, g):
            for u in range(2):
                first = K_PASS * g + 2 * P * u
                nc.sync.dma_start(
                    out=w_raw[half][:, g, 2 * u : 2 * u + 2, :],
                    in_=W3_w[first : first + 2 * P, N_TILE * half : N_TILE * (half + 1)].rearrange(
                        "(p v) c -> p v c", v=2
                    ),
                )

        def load_h2(c):
            for first in range(0, CHUNK * K, LOAD * K):
                nc.sync.dma_start(
                    out=h2_in[c][:, first : first + LOAD * K],
                    in_=h2_rows[:, CHUNK * K * c + first : CHUNK * K * c + first + LOAD * K],
                )

        for g in range(PASSES):
            load_w(0, g)
        for c in range(CHUNKS):
            load_h2(c)
            if 0 <= c - 1 < PASSES:
                load_w(1, c - 1)
        hv = keep.tile([P, H], BF16)
        nc.sync.dma_start(out=hv[:], in_=hv_rows)

        ident = keep.tile([P, P], F32)
        make_identity(nc, ident[:])
        mask_f32 = keep.tile([P, EDGES], F32)
        nc.vector.tensor_copy(out=mask_f32[:], in_=mask_bf[:])
        gates = keep.tile([P, EDGES, P], F32)

        def make_gates(c):
            for e in range(CHUNK * c, CHUNK * (c + 1)):
                nc.vector.tensor_scalar(
                    out=gates[:, e, :], in0=ident[:], scalar1=mask_f32[:, e : e + 1], scalar2=None, op0=ALU.mult
                )

        make_gates(0)

        count = keep.tile([P, 1], F32)
        nc.vector.reduce_sum(out=count[:], in_=mask_f32[:], axis=mybir.AxisListType.X)
        count30 = keep.tile([P, 1], F32)
        nc.vector.tensor_scalar(out=count30[:], in0=count[:], scalar1=1.0 / SCALE, scalar2=None, op0=ALU.mult)

        bias_all = [acc_pool.tile([P, N_TILE], F32, name="bias_all%d" % half, tag="late%d" % half) for half in range(HALVES)]
        for half in range(HALVES):
            nc.tensor.matmul(
                out=bias_all[half][:],
                lhsT=ones[:],
                rhs=bias_rows[:, N_TILE * half : N_TILE * (half + 1)],
                start=True,
                stop=True,
            )

        w_grouped = [
            keep.tile([P, PASSES, N_TILE, PACK], BF16, name="w_grouped%d" % half, align_bytes=64)
            for half in range(HALVES)
        ]
        w_codes = keep.tile([P, PASSES, H], U32, align_bytes=64)
        w_scales = keep.tile([P, PASSES, H], U8, align_bytes=64)

        def regroup_w(half, g):
            nc.vector.tensor_copy(
                out=w_grouped[half][:, g].rearrange("p (c i) t -> p c t i", i=4),
                in_=w_raw[half][:, g].rearrange("p t (c i) -> p c t i", i=4),
            )

        def quantise_w(half, g):
            cols = slice(N_TILE * half, N_TILE * (half + 1))
            nc.vector.quantize_mx(
                out=w_codes[:, g, cols].bitcast(FP8X4),
                scales=w_scales[:, g, cols],
                in_=w_grouped[half][:, g].rearrange("p c t -> p (c t)"),
            )

        h2_grouped = [keep.tile([P, CHUNK * K], BF16, name="h2_grouped%d" % c, align_bytes=64) for c in range(CHUNKS)]
        h2_codes = keep.tile([P, EDGES, PASSES * P], U32, align_bytes=64)
        h2_scales = keep.tile([P, EDGES, PASSES * P], U8, align_bytes=64)

        def quantise_h2(c):
            words_in = h2_in[c][:].bitcast(F32)
            words_out = h2_grouped[c][:].bitcast(F32).rearrange(
                "p (e g n u) -> p e g n u", e=CHUNK, g=PASSES, u=2
            )
            for i in range(CHUNK):
                e = CHUNK * c + i
                turned = turn_pool.tile([P, PLANES, P], F32)
                for j in range(PLANES):
                    first = (PLANES * i + j) * P
                    nc.tensor.transpose(turned[:, j, :], words_in[:, first : first + P], gates[:, e, :])
                nc.scalar.copy(out=words_out[:, i], in_=turned[:].rearrange("p (g u) n -> p g n u", u=2))
                nc.vector.quantize_mx(
                    out=h2_codes[:, e, :].bitcast(FP8X4),
                    scales=h2_scales[:, e, :],
                    in_=h2_grouped[c][:, K * i : K * (i + 1)],
                )

        def multiply(acc, group, edges):
            first, width = group
            for e in edges:
                for g in range(PASSES):
                    nc.tensor.matmul_mx(
                        out=acc[:],
                        lhsT=h2_codes[:, e, P * g : P * (g + 1)].bitcast(FP8X4),
                        lhsT_scale=h2_scales[:, e, P * g : P * (g + 1)],
                        rhs=w_codes[:, g, first : first + width].bitcast(FP8X4),
                        rhs_scale=w_scales[:, g, first : first + width],
                        start=(e == 0 and g == 0),
                        stop=(e == EDGES - 1 and g == PASSES - 1),
                    )

        base = keep.tile([P, H], F32)
        result = keep.tile([P, H], F32)

        def finish(acc, group):
            first, width = group
            cols = slice(first, first + width)
            nc.vector.scalar_tensor_tensor(
                out=result[:, cols], in0=acc[:], scalar=1.0 / SCALE, in1=base[:, cols], op0=ALU.mult, op1=ALU.add
            )
            nc.sync.dma_start(out=out_rows[:, cols], in_=result[:, cols])

        for g in range(PASSES):
            regroup_w(0, g)
        for g in range(PASSES):
            quantise_w(0, g)
        acc_first = acc_pool.tile([P, GROUPS[0][1]], F32)
        for c in range(CHUNKS):
            if c + 1 < CHUNKS:
                make_gates(c + 1)
            quantise_h2(c)
            if 0 <= c - 1 < PASSES:
                regroup_w(1, c - 1)
                quantise_w(1, c - 1)
            multiply(acc_first, GROUPS[0], range(max(0, CHUNK * c - LAG), CHUNK * (c + 1) - LAG))
        multiply(acc_first, GROUPS[0], range(EDGES - LAG, EDGES))

        for half in range(HALVES):
            cols = slice(N_TILE * half, N_TILE * (half + 1))
            nc.vector.scalar_tensor_tensor(
                out=base[:, cols], in0=bias_all[half][:], scalar=count30[:, 0:1], in1=hv[:, cols], op0=ALU.mult, op1=ALU.add
            )
        finish(acc_first, GROUPS[0])

        for late, group in enumerate(GROUPS[1:]):
            acc_late = acc_pool.tile([P, group[1]], F32, tag="late%d" % late)
            multiply(acc_late, group, range(EDGES))
            finish(acc_late, group)
